import numpy as np
import ml_dtypes


def mxq(x, axis, fmt="e4m3"):
    dtype, down = {"e4m3": (ml_dtypes.float8_e4m3fn, 7), "e5m2": (ml_dtypes.float8_e5m2, 14)}[fmt]
    v = np.moveaxis(np.asarray(x, np.float32).astype(ml_dtypes.bfloat16).astype(np.float64), axis, -1)
    blocks = v.reshape(v.shape[:-1] + (-1, 32))
    amax = np.abs(blocks).max(-1, keepdims=True)
    byte = np.maximum(np.where(amax > 0, np.frexp(amax)[1] - 1 + 127, 0) - down, 1)
    scale = np.exp2(byte - 127.0)
    codes = (blocks / scale).astype(np.float32).astype(dtype).astype(np.float64)
    return np.moveaxis((codes * scale).reshape(v.shape), -1, axis)


WIDE = False


def mx_kscale(k):
    if not WIDE:
        return np.ones(k)
    levels = np.array([10, -10, 5, -5, 0])
    a = np.random.permutation(np.resize(levels, k // 512 * 4)).reshape(k // 512, 4)
    idx = np.arange(k)
    return np.exp2(a[idx // 512, idx % 128 // 32])


BF16 = ml_dtypes.bfloat16


def bf(x):
    return np.asarray(x, np.float32).astype(BF16)


def f64(x):
    return np.asarray(x).astype(np.float64)


B, T, D, E, H, L = 128, 10, 1024, 128, 128, 2
TM = T - L
F = H + L * D + 1


def setup_inputs():
    s = mx_kscale(D)
    we = np.random.standard_normal((D, H)) / np.sqrt(H)
    wy = np.random.standard_normal((D, L, D)) * 0.7 / np.sqrt(L * D) / s
    wx = np.random.standard_normal((D, 1)) * 0.5 / s[:, None]
    return {"x": bf(np.random.standard_normal((B, T, D)) * s),
            "emb": bf(np.random.standard_normal((B, H)) * 0.5),
            "Wg": bf(np.concatenate([we, wy.reshape(D, L * D), wx], axis=1)),
            "bg": bf(np.random.standard_normal(D) * 0.3)}


def reference(x, emb, Wg, bg):
    xf = f64(x)
    Wy = f64(Wg)[:, H:H + L * D].reshape(D, L, D)
    wx = f64(Wg)[:, -1]
    ctx = f64(emb) @ f64(Wg)[:, :H].T
    xq = mxq(xf[:, :T - 1, :], 2, "e4m3")
    wq = mxq(Wy, 2, "e4m3")
    lag = sum((xq[:, l:TM + l, :] @ wq[:, l, :].T) for l in range(L))
    return ctx[:, None, :] + lag + xf[:, L:, :] * wx + f64(bg)

@@ -1,0 +1,188 @@
+from contextlib import ExitStack
+
+import concourse.mybir as mybir
+from concourse.masks import make_identity
+
+F32 = mybir.dt.float32
+BF16 = mybir.dt.bfloat16
+I32 = mybir.dt.int32
+U32 = mybir.dt.uint32
+U8 = mybir.dt.uint8
+FP8X4 = mybir.dt.float8_e4m3fn_x4
+ADD = mybir.AluOpType.add
+MULT = mybir.AluOpType.mult
+
+P = 128
+B, T, D, H, L = 128, 10, 1024, 128, 2
+TM = T - L
+F = H + L * D + 1
+F_PAD = 2192
+
+PACK = 4
+K_PASS = P * PACK
+PASSES = D // K_PASS
+HALVES = 2
+PASS_WORDS = K_PASS // 2
+
+BANK = 512
+D_TILE = 256
+D_TILES = D // D_TILE
+BLOCKS = D_TILE // P
+T_BANK = BANK // D_TILE
+X_LOAD = 2
+
+FLOPS = 2 * B * TM * D * L * D + 2 * B * D * H
+
+
+def tile_npchangetransitionprior_pa_kernel(tc, x, emb, Wg, bg, out):
+    nc = tc.nc
+    with ExitStack() as stack:
+        keep = stack.enter_context(tc.tile_pool(name="keep", bufs=1))
+        x_stage = stack.enter_context(tc.tile_pool(name="x_stage", bufs=3))
+        w_stage = stack.enter_context(tc.tile_pool(name="w_stage", bufs=2))
+        psum_stage = stack.enter_context(tc.psum_pool(name="psum_stage", bufs=4))
+        psum_lag = stack.enter_context(tc.psum_pool(name="psum_lag", bufs=2))
+        psum_keep = stack.enter_context(tc.psum_pool(name="psum_keep", bufs=1))
+
+        ident_f32 = keep.tile([P, P], F32)
+        make_identity(nc, ident_f32[:])
+        ident_bf16 = keep.tile([P, P], BF16)
+        make_identity(nc, ident_bf16[:])
+        ones = keep.tile([P, P], BF16)
+        nc.vector.memset(ones[:], 1.0)
+        bias_rows = keep.tile([P, D], BF16)
+        nc.vector.memset(bias_rows[:].bitcast(I32), 0)
+
+        emb_sb = keep.tile([P, H], BF16)
+        x_sb = keep.tile([P, T, D], BF16)
+        w_sb = keep.tile([P, D // P, F_PAD], BF16)
+
+        def load_w_tile(dtile):
+            for block in range(dtile * BLOCKS, (dtile + 1) * BLOCKS):
+                nc.sync.dma_start(out=w_sb[:, block, 0:F], in_=Wg[block * P : (block + 1) * P, :])
+
+        nc.sync.dma_start(out=emb_sb[:], in_=emb)
+        nc.sync.dma_start(out=bias_rows[0:1, :], in_=bg.rearrange("(o d) -> o d", o=1))
+        load_w_tile(0)
+        for s in range(0, T, X_LOAD):
+            nc.sync.dma_start(out=x_sb[:, s : s + X_LOAD, :], in_=x[:, s : s + X_LOAD, :])
+        for dtile in range(1, D_TILES):
+            load_w_tile(dtile)
+
+        x_codes = keep.tile([P, T - 1, PASSES * B], U32, align_bytes=64)
+        x_scales = keep.tile([P, T - 1, PASSES * B], U8, align_bytes=64)
+        w_codes = keep.tile([P, D_TILES, L * PASSES * D_TILE], U32, align_bytes=64)
+        w_scales = keep.tile([P, D_TILES, L * PASSES * D_TILE], U8, align_bytes=64)
+        embT = keep.tile([P, B], BF16)
+        weT = keep.tile([P, D], BF16)
+        wx_rows = keep.tile([P, D], F32)
+        context = [psum_keep.tile([P, BANK], F32, name="context%d" % i) for i in range(D // BANK)]
+        res = keep.tile([P, TM, D], F32)
+
+        def word_transposes(bank, words, first_word):
+            for g in range(PASSES):
+                for u in range(HALVES):
+                    start = first_word + g * PASS_WORDS + u * P
+                    nc.tensor.transpose(bank[:, g, u, :], words[:, start : start + P], ident_f32[:])
+
+        def quantise_x_step(s):
+            bank = psum_stage.tile([P, PASSES, HALVES, B], F32, tag="stage")
+            word_transposes(bank, x_sb[:, s, :].bitcast(F32), 0)
+            grouped = x_stage.tile([P, PASSES, B, PACK], BF16, align_bytes=64)
+            nc.scalar.copy(out=grouped[:].bitcast(F32), in_=bank[:].rearrange("p g u b -> p g b u"))
+            nc.vector.quantize_mx(
+                out=x_codes[:, s, :].bitcast(FP8X4),
+                scales=x_scales[:, s, :],
+                in_=grouped[:].rearrange("p g b j -> p (g b j)"),
+            )
+
+        def quantise_w_tile(dtile):
+            grouped = w_stage.tile([P, L, PASSES, D_TILE, PACK], BF16, align_bytes=64)
+            grouped_words = grouped[:].bitcast(F32)
+            for i in range(BLOCKS):
+                words = w_sb[:, dtile * BLOCKS + i, :].bitcast(F32)
+                for l in range(L):
+                    bank = psum_stage.tile([P, PASSES, HALVES, P], F32, tag="stage")
+                    word_transposes(bank, words, (H + l * D) // 2)
+                    nc.scalar.copy(
+                        out=grouped_words[:, l, :, i * P : (i + 1) * P, :],
+                        in_=bank[:].rearrange("p g u d -> p g d u"),
+                    )
+            nc.vector.quantize_mx(
+                out=w_codes[:, dtile, :].bitcast(FP8X4),
+                scales=w_scales[:, dtile, :],
+                in_=grouped[:].rearrange("p l g d j -> p (l g d j)"),
+            )
+
+        def context_columns(dtile):
+            first = dtile * D_TILE
+            return context[first // BANK][:, first % BANK : first % BANK + D_TILE]
+
+        def plain_terms(dtile):
+            cols = slice(dtile * D_TILE, (dtile + 1) * D_TILE)
+            weT_ps = psum_stage.tile([P, D_TILE], BF16, tag="stage")
+            wx_ps = psum_stage.tile([P, D_TILE], F32, tag="stage")
+            for i in range(BLOCKS):
+                block = dtile * BLOCKS + i
+                part = slice(i * P, (i + 1) * P)
+                nc.tensor.transpose(weT_ps[:, part], w_sb[:, block, 0:H], ident_bf16[:])
+                nc.tensor.matmul(
+                    wx_ps[:, part],
+                    lhsT=w_sb[:, block, F - 1 : F].to_broadcast([P, P]),
+                    rhs=ident_bf16[:],
+                    start=True,
+                    stop=True,
+                )
+            nc.scalar.copy(out=weT[:, cols], in_=weT_ps[:])
+            nc.scalar.copy(out=wx_rows[:, cols], in_=wx_ps[:])
+            nc.tensor.matmul(context_columns(dtile), lhsT=embT[:], rhs=weT[:, cols], start=True, stop=False)
+            nc.tensor.matmul(context_columns(dtile), lhsT=ones[:], rhs=bias_rows[:, cols], start=False, stop=True)
+            nc.vector.tensor_tensor(
+                out=res[:, :, cols],
+                in0=x_sb[:, L:T, cols],
+                in1=wx_rows[:, cols].unsqueeze(1).to_broadcast([P, TM, D_TILE]),
+                op=MULT,
+            )
+            nc.vector.tensor_tensor(
+                out=res[:, :, cols],
+                in0=res[:, :, cols],
+                in1=context_columns(dtile).unsqueeze(1).to_broadcast([P, TM, D_TILE]),
+                op=ADD,
+            )
+
+        def lag_terms(dtile, first_t):
+            cols = slice(dtile * D_TILE, (dtile + 1) * D_TILE)
+            steps = slice(first_t, first_t + T_BANK)
+            sums = psum_lag.tile([P, T_BANK, D_TILE], F32)
+            for i in range(T_BANK):
+                for l in range(L):
+                    for g in range(PASSES):
+                        series = slice(g * B, (g + 1) * B)
+                        latents = slice((l * PASSES + g) * D_TILE, (l * PASSES + g + 1) * D_TILE)
+                        nc.tensor.matmul_mx(
+                            out=sums[:, i, :],
+                            lhsT=x_codes[:, first_t + i + l, series].bitcast(FP8X4),
+                            lhsT_scale=x_scales[:, first_t + i + l, series],
+                            rhs=w_codes[:, dtile, latents].bitcast(FP8X4),
+                            rhs_scale=w_scales[:, dtile, latents],
+                            start=(l == 0 and g == 0),
+                            stop=(l == L - 1 and g == PASSES - 1),
+                        )
+            nc.vector.tensor_tensor(out=res[:, steps, cols], in0=sums[:], in1=res[:, steps, cols], op=ADD)
+            nc.sync.dma_start(out=out[:, steps, cols], in_=res[:, steps, cols])
+
+        embT_ps = psum_stage.tile([P, B], BF16, tag="stage")
+        nc.tensor.transpose(embT_ps[:], emb_sb[:], ident_bf16[:])
+        nc.scalar.copy(out=embT[:], in_=embT_ps[:])
+
+        quantise_w_tile(0)
+        for s in range(T - 1):
+            quantise_x_step(s)
+        plain_terms(0)
+        for dtile in range(D_TILES):
+            lag_terms(dtile, 0)
+            if dtile + 1 < D_TILES:
+                quantise_w_tile(dtile + 1)
+                plain_terms(dtile + 1)
+            for first_t in range(T_BANK, TM, T_BANK):
+                lag_terms(dtile, first_t)

@@ -30,6 +30,7 @@ D_TILES = D // D_TILE
 BLOCKS = D_TILE // P
 T_BANK = BANK // D_TILE
 X_LOAD = 2
+PLAIN_STEPS = 4
 
 FLOPS = 2 * B * TM * D * L * D + 2 * B * D * H
 
@@ -118,7 +119,7 @@ def tile_npchangetransitionprior_pa_kernel(tc, x, emb, Wg, bg, out):
             first = dtile * D_TILE
             return context[first // BANK][:, first % BANK : first % BANK + D_TILE]
 
-        def plain_terms(dtile):
+        def context_term(dtile):
             cols = slice(dtile * D_TILE, (dtile + 1) * D_TILE)
             weT_ps = psum_stage.tile([P, D_TILE], BF16, tag="stage")
             wx_ps = psum_stage.tile([P, D_TILE], F32, tag="stage")
@@ -137,16 +138,20 @@ def tile_npchangetransitionprior_pa_kernel(tc, x, emb, Wg, bg, out):
             nc.scalar.copy(out=wx_rows[:, cols], in_=wx_ps[:])
             nc.tensor.matmul(context_columns(dtile), lhsT=embT[:], rhs=weT[:, cols], start=True, stop=False)
             nc.tensor.matmul(context_columns(dtile), lhsT=ones[:], rhs=bias_rows[:, cols], start=False, stop=True)
-            nc.vector.tensor_tensor(
-                out=res[:, :, cols],
-                in0=x_sb[:, L:T, cols],
-                in1=wx_rows[:, cols].unsqueeze(1).to_broadcast([P, TM, D_TILE]),
+
+        def plain_terms(dtile, first_t):
+            cols = slice(dtile * D_TILE, (dtile + 1) * D_TILE)
+            steps = slice(first_t, first_t + PLAIN_STEPS)
+            nc.gpsimd.tensor_tensor(
+                out=res[:, steps, cols],
+                in0=x_sb[:, L + first_t : L + first_t + PLAIN_STEPS, cols],
+                in1=wx_rows[:, cols].unsqueeze(1).to_broadcast([P, PLAIN_STEPS, D_TILE]),
                 op=MULT,
             )
             nc.vector.tensor_tensor(
-                out=res[:, :, cols],
-                in0=res[:, :, cols],
-                in1=context_columns(dtile).unsqueeze(1).to_broadcast([P, TM, D_TILE]),
+                out=res[:, steps, cols],
+                in0=res[:, steps, cols],
+                in1=context_columns(dtile).unsqueeze(1).to_broadcast([P, PLAIN_STEPS, D_TILE]),
                 op=ADD,
             )
 
@@ -176,13 +181,17 @@ def tile_npchangetransitionprior_pa_kernel(tc, x, emb, Wg, bg, out):
         nc.scalar.copy(out=embT[:], in_=embT_ps[:])
 
         quantise_w_tile(0)
+        context_term(0)
         for s in range(T - 1):
             quantise_x_step(s)
-        plain_terms(0)
+        for first_t in range(0, TM, PLAIN_STEPS):
+            plain_terms(0, first_t)
         for dtile in range(D_TILES):
             lag_terms(dtile, 0)
             if dtile + 1 < D_TILES:
                 quantise_w_tile(dtile + 1)
-                plain_terms(dtile + 1)
+                context_term(dtile + 1)
+                for first_t in range(0, TM, PLAIN_STEPS):
+                    plain_terms(dtile + 1, first_t)
             for first_t in range(T_BANK, TM, T_BANK):
                 lag_terms(dtile, first_t)

@@ -30,7 +30,6 @@ D_TILES = D // D_TILE
 BLOCKS = D_TILE // P
 T_BANK = BANK // D_TILE
 X_LOAD = 2
-PLAIN_STEPS = 4
 
 FLOPS = 2 * B * TM * D * L * D + 2 * B * D * H
 
@@ -41,9 +40,8 @@ def tile_npchangetransitionprior_pa_kernel(tc, x, emb, Wg, bg, out):
         keep = stack.enter_context(tc.tile_pool(name="keep", bufs=1))
         x_stage = stack.enter_context(tc.tile_pool(name="x_stage", bufs=3))
         w_stage = stack.enter_context(tc.tile_pool(name="w_stage", bufs=2))
-        psum_stage = stack.enter_context(tc.psum_pool(name="psum_stage", bufs=4))
-        psum_lag = stack.enter_context(tc.psum_pool(name="psum_lag", bufs=2))
-        psum_keep = stack.enter_context(tc.psum_pool(name="psum_keep", bufs=1))
+        psum_stage = stack.enter_context(tc.psum_pool(name="psum_stage", bufs=5))
+        psum_lag = stack.enter_context(tc.psum_pool(name="psum_lag", bufs=3))
 
         ident_f32 = keep.tile([P, P], F32)
         make_identity(nc, ident_f32[:])
@@ -76,8 +74,6 @@ def tile_npchangetransitionprior_pa_kernel(tc, x, emb, Wg, bg, out):
         w_scales = keep.tile([P, D_TILES, L * PASSES * D_TILE], U8, align_bytes=64)
         embT = keep.tile([P, B], BF16)
         weT = keep.tile([P, D], BF16)
-        wx_rows = keep.tile([P, D], F32)
-        context = [psum_keep.tile([P, BANK], F32, name="context%d" % i) for i in range(D // BANK)]
         res = keep.tile([P, TM, D], F32)
 
         def word_transposes(bank, words, first_word):
@@ -115,43 +111,39 @@ def tile_npchangetransitionprior_pa_kernel(tc, x, emb, Wg, bg, out):
                 in_=grouped[:].rearrange("p l g d j -> p (l g d j)"),
             )
 
-        def context_columns(dtile):
-            first = dtile * D_TILE
-            return context[first // BANK][:, first % BANK : first % BANK + D_TILE]
-
-        def context_term(dtile):
+        def row_terms(dtile):
             cols = slice(dtile * D_TILE, (dtile + 1) * D_TILE)
             weT_ps = psum_stage.tile([P, D_TILE], BF16, tag="stage")
-            wx_ps = psum_stage.tile([P, D_TILE], F32, tag="stage")
+            rows = psum_stage.tile([P, 2, D_TILE], F32, tag="stage")
             for i in range(BLOCKS):
                 block = dtile * BLOCKS + i
                 part = slice(i * P, (i + 1) * P)
                 nc.tensor.transpose(weT_ps[:, part], w_sb[:, block, 0:H], ident_bf16[:])
                 nc.tensor.matmul(
-                    wx_ps[:, part],
+                    rows[:, 0, part],
                     lhsT=w_sb[:, block, F - 1 : F].to_broadcast([P, P]),
                     rhs=ident_bf16[:],
                     start=True,
                     stop=True,
                 )
             nc.scalar.copy(out=weT[:, cols], in_=weT_ps[:])
-            nc.scalar.copy(out=wx_rows[:, cols], in_=wx_ps[:])
-            nc.tensor.matmul(context_columns(dtile), lhsT=embT[:], rhs=weT[:, cols], start=True, stop=False)
-            nc.tensor.matmul(context_columns(dtile), lhsT=ones[:], rhs=bias_rows[:, cols], start=False, stop=True)
+            nc.tensor.matmul(rows[:, 1, :], lhsT=embT[:], rhs=weT[:, cols], start=True, stop=False)
+            nc.tensor.matmul(rows[:, 1, :], lhsT=ones[:], rhs=bias_rows[:, cols], start=False, stop=True)
+            return rows
 
-        def plain_terms(dtile, first_t):
+        def plain_terms(dtile, first_t, rows):
             cols = slice(dtile * D_TILE, (dtile + 1) * D_TILE)
-            steps = slice(first_t, first_t + PLAIN_STEPS)
-            nc.gpsimd.tensor_tensor(
+            steps = slice(first_t, first_t + T_BANK)
+            nc.vector.tensor_tensor(
                 out=res[:, steps, cols],
-                in0=x_sb[:, L + first_t : L + first_t + PLAIN_STEPS, cols],
-                in1=wx_rows[:, cols].unsqueeze(1).to_broadcast([P, PLAIN_STEPS, D_TILE]),
+                in0=x_sb[:, L + first_t : L + first_t + T_BANK, cols],
+                in1=rows[:, 0:1, :].to_broadcast([P, T_BANK, D_TILE]),
                 op=MULT,
             )
             nc.vector.tensor_tensor(
                 out=res[:, steps, cols],
                 in0=res[:, steps, cols],
-                in1=context_columns(dtile).unsqueeze(1).to_broadcast([P, PLAIN_STEPS, D_TILE]),
+                in1=rows[:, 1:2, :].to_broadcast([P, T_BANK, D_TILE]),
                 op=ADD,
             )
 
@@ -181,17 +173,22 @@ def tile_npchangetransitionprior_pa_kernel(tc, x, emb, Wg, bg, out):
         nc.scalar.copy(out=embT[:], in_=embT_ps[:])
 
         quantise_w_tile(0)
-        context_term(0)
-        for s in range(T - 1):
+        rows = row_terms(0)
+        for s in range(L):
             quantise_x_step(s)
-        for first_t in range(0, TM, PLAIN_STEPS):
-            plain_terms(0, first_t)
+        for first_t in range(0, TM, T_BANK):
+            for s in range(first_t + L, min(first_t + L + T_BANK, T - 1)):
+                quantise_x_step(s)
+            plain_terms(0, first_t, rows)
         for dtile in range(D_TILES):
+            more = dtile + 1 < D_TILES
             lag_terms(dtile, 0)
-            if dtile + 1 < D_TILES:
+            if more:
                 quantise_w_tile(dtile + 1)
-                context_term(dtile + 1)
-                for first_t in range(0, TM, PLAIN_STEPS):
-                    plain_terms(dtile + 1, first_t)
+                rows = row_terms(dtile + 1)
             for first_t in range(T_BANK, TM, T_BANK):
+                if more:
+                    plain_terms(dtile + 1, first_t - T_BANK, rows)
                 lag_terms(dtile, first_t)
+            if more:
+                plain_terms(dtile + 1, TM - T_BANK, rows)

@@ -29,7 +29,8 @@ D_TILE = 256
 D_TILES = D // D_TILE
 BLOCKS = D_TILE // P
 T_BANK = BANK // D_TILE
-X_LOAD = 2
+X_LOAD = T_BANK
+X_ORDER = [L] + [s for s in range(0, T, X_LOAD) if s != L]
 
 FLOPS = 2 * B * TM * D * L * D + 2 * B * D * H
 
@@ -42,6 +43,7 @@ def tile_npchangetransitionprior_pa_kernel(tc, x, emb, Wg, bg, out):
         w_stage = stack.enter_context(tc.tile_pool(name="w_stage", bufs=2))
         psum_stage = stack.enter_context(tc.psum_pool(name="psum_stage", bufs=5))
         psum_lag = stack.enter_context(tc.psum_pool(name="psum_lag", bufs=3))
+        stack.enter_context(tc.manual_schedule())
 
         ident_f32 = keep.tile([P, P], F32)
         make_identity(nc, ident_f32[:])
@@ -63,7 +65,7 @@ def tile_npchangetransitionprior_pa_kernel(tc, x, emb, Wg, bg, out):
         nc.sync.dma_start(out=emb_sb[:], in_=emb)
         nc.sync.dma_start(out=bias_rows[0:1, :], in_=bg.rearrange("(o d) -> o d", o=1))
         load_w_tile(0)
-        for s in range(0, T, X_LOAD):
+        for s in X_ORDER:
             nc.sync.dma_start(out=x_sb[:, s : s + X_LOAD, :], in_=x[:, s : s + X_LOAD, :])
         for dtile in range(1, D_TILES):
             load_w_tile(dtile)
@@ -131,25 +133,26 @@ def tile_npchangetransitionprior_pa_kernel(tc, x, emb, Wg, bg, out):
             nc.tensor.matmul(rows[:, 1, :], lhsT=ones[:], rhs=bias_rows[:, cols], start=False, stop=True)
             return rows
 
-        def plain_terms(dtile, first_t, rows):
-            cols = slice(dtile * D_TILE, (dtile + 1) * D_TILE)
-            steps = slice(first_t, first_t + T_BANK)
+        def piece(dtile, first_t):
+            return res[:, first_t : first_t + T_BANK, dtile * D_TILE : (dtile + 1) * D_TILE]
+
+        def own_latent_term(dtile, first_t, rows):
             nc.vector.tensor_tensor(
-                out=res[:, steps, cols],
-                in0=x_sb[:, L + first_t : L + first_t + T_BANK, cols],
+                out=piece(dtile, first_t),
+                in0=x_sb[:, L + first_t : L + first_t + T_BANK, dtile * D_TILE : (dtile + 1) * D_TILE],
                 in1=rows[:, 0:1, :].to_broadcast([P, T_BANK, D_TILE]),
                 op=MULT,
             )
+
+        def add_context(dtile, first_t, rows):
             nc.vector.tensor_tensor(
-                out=res[:, steps, cols],
-                in0=res[:, steps, cols],
+                out=piece(dtile, first_t),
+                in0=piece(dtile, first_t),
                 in1=rows[:, 1:2, :].to_broadcast([P, T_BANK, D_TILE]),
                 op=ADD,
             )
 
-        def lag_terms(dtile, first_t):
-            cols = slice(dtile * D_TILE, (dtile + 1) * D_TILE)
-            steps = slice(first_t, first_t + T_BANK)
+        def lag_sums(dtile, first_t):
             sums = psum_lag.tile([P, T_BANK, D_TILE], F32)
             for i in range(T_BANK):
                 for l in range(L):
@@ -165,30 +168,38 @@ def tile_npchangetransitionprior_pa_kernel(tc, x, emb, Wg, bg, out):
                             start=(l == 0 and g == 0),
                             stop=(l == L - 1 and g == PASSES - 1),
                         )
-            nc.vector.tensor_tensor(out=res[:, steps, cols], in0=sums[:], in1=res[:, steps, cols], op=ADD)
-            nc.sync.dma_start(out=out[:, steps, cols], in_=res[:, steps, cols])
+            return sums
+
+        def add_lag_sums_and_store(dtile, first_t, sums):
+            nc.vector.tensor_tensor(out=piece(dtile, first_t), in0=sums[:], in1=piece(dtile, first_t), op=ADD)
+            nc.sync.dma_start(
+                out=out[:, first_t : first_t + T_BANK, dtile * D_TILE : (dtile + 1) * D_TILE],
+                in_=piece(dtile, first_t),
+            )
 
         embT_ps = psum_stage.tile([P, B], BF16, tag="stage")
         nc.tensor.transpose(embT_ps[:], emb_sb[:], ident_bf16[:])
         nc.scalar.copy(out=embT[:], in_=embT_ps[:])
 
-        quantise_w_tile(0)
         rows = row_terms(0)
-        for s in range(L):
-            quantise_x_step(s)
-        for first_t in range(0, TM, T_BANK):
-            for s in range(first_t + L, min(first_t + L + T_BANK, T - 1)):
-                quantise_x_step(s)
-            plain_terms(0, first_t, rows)
+        quantise_w_tile(0)
+        for s in X_ORDER:
+            if s >= L:
+                own_latent_term(0, s - L, rows)
+            for step in range(s, min(s + X_LOAD, T - 1)):
+                quantise_x_step(step)
+            if s >= L:
+                add_context(0, s - L, rows)
+
         for dtile in range(D_TILES):
             more = dtile + 1 < D_TILES
-            lag_terms(dtile, 0)
             if more:
                 quantise_w_tile(dtile + 1)
                 rows = row_terms(dtile + 1)
-            for first_t in range(T_BANK, TM, T_BANK):
+            for first_t in range(0, TM, T_BANK):
+                sums = lag_sums(dtile, first_t)
                 if more:
-                    plain_terms(dtile + 1, first_t - T_BANK, rows)
-                lag_terms(dtile, first_t)
-            if more:
-                plain_terms(dtile + 1, TM - T_BANK, rows)
+                    own_latent_term(dtile + 1, first_t, rows)
+                add_lag_sums_and_store(dtile, first_t, sums)
+                if more:
+                    add_context(dtile + 1, first_t, rows)

@@ -41,9 +41,8 @@ def tile_npchangetransitionprior_pa_kernel(tc, x, emb, Wg, bg, out):
         keep = stack.enter_context(tc.tile_pool(name="keep", bufs=1))
         x_stage = stack.enter_context(tc.tile_pool(name="x_stage", bufs=3))
         w_stage = stack.enter_context(tc.tile_pool(name="w_stage", bufs=2))
-        psum_stage = stack.enter_context(tc.psum_pool(name="psum_stage", bufs=5))
-        psum_lag = stack.enter_context(tc.psum_pool(name="psum_lag", bufs=3))
-        stack.enter_context(tc.manual_schedule())
+        psum_stage = stack.enter_context(tc.psum_pool(name="psum_stage", bufs=4))
+        psum_lag = stack.enter_context(tc.psum_pool(name="psum_lag", bufs=4))
 
         ident_f32 = keep.tile([P, P], F32)
         make_identity(nc, ident_f32[:])
@@ -133,26 +132,25 @@ def tile_npchangetransitionprior_pa_kernel(tc, x, emb, Wg, bg, out):
             nc.tensor.matmul(rows[:, 1, :], lhsT=ones[:], rhs=bias_rows[:, cols], start=False, stop=True)
             return rows
 
-        def piece(dtile, first_t):
-            return res[:, first_t : first_t + T_BANK, dtile * D_TILE : (dtile + 1) * D_TILE]
-
-        def own_latent_term(dtile, first_t, rows):
+        def plain_terms(dtile, first_t, rows):
+            cols = slice(dtile * D_TILE, (dtile + 1) * D_TILE)
+            steps = slice(first_t, first_t + T_BANK)
             nc.vector.tensor_tensor(
-                out=piece(dtile, first_t),
-                in0=x_sb[:, L + first_t : L + first_t + T_BANK, dtile * D_TILE : (dtile + 1) * D_TILE],
+                out=res[:, steps, cols],
+                in0=x_sb[:, L + first_t : L + first_t + T_BANK, cols],
                 in1=rows[:, 0:1, :].to_broadcast([P, T_BANK, D_TILE]),
                 op=MULT,
             )
-
-        def add_context(dtile, first_t, rows):
             nc.vector.tensor_tensor(
-                out=piece(dtile, first_t),
-                in0=piece(dtile, first_t),
+                out=res[:, steps, cols],
+                in0=res[:, steps, cols],
                 in1=rows[:, 1:2, :].to_broadcast([P, T_BANK, D_TILE]),
                 op=ADD,
             )
 
-        def lag_sums(dtile, first_t):
+        def lag_terms(dtile, first_t):
+            cols = slice(dtile * D_TILE, (dtile + 1) * D_TILE)
+            steps = slice(first_t, first_t + T_BANK)
             sums = psum_lag.tile([P, T_BANK, D_TILE], F32)
             for i in range(T_BANK):
                 for l in range(L):
@@ -168,14 +166,8 @@ def tile_npchangetransitionprior_pa_kernel(tc, x, emb, Wg, bg, out):
                             start=(l == 0 and g == 0),
                             stop=(l == L - 1 and g == PASSES - 1),
                         )
-            return sums
-
-        def add_lag_sums_and_store(dtile, first_t, sums):
-            nc.vector.tensor_tensor(out=piece(dtile, first_t), in0=sums[:], in1=piece(dtile, first_t), op=ADD)
-            nc.sync.dma_start(
-                out=out[:, first_t : first_t + T_BANK, dtile * D_TILE : (dtile + 1) * D_TILE],
-                in_=piece(dtile, first_t),
-            )
+            nc.vector.tensor_tensor(out=res[:, steps, cols], in0=sums[:], in1=res[:, steps, cols], op=ADD)
+            nc.sync.dma_start(out=out[:, steps, cols], in_=res[:, steps, cols])
 
         embT_ps = psum_stage.tile([P, B], BF16, tag="stage")
         nc.tensor.transpose(embT_ps[:], emb_sb[:], ident_bf16[:])
@@ -185,21 +177,18 @@ def tile_npchangetransitionprior_pa_kernel(tc, x, emb, Wg, bg, out):
         quantise_w_tile(0)
         for s in X_ORDER:
             if s >= L:
-                own_latent_term(0, s - L, rows)
+                plain_terms(0, s - L, rows)
             for step in range(s, min(s + X_LOAD, T - 1)):
                 quantise_x_step(step)
-            if s >= L:
-                add_context(0, s - L, rows)
-
         for dtile in range(D_TILES):
             more = dtile + 1 < D_TILES
+            lag_terms(dtile, 0)
             if more:
                 quantise_w_tile(dtile + 1)
                 rows = row_terms(dtile + 1)
-            for first_t in range(0, TM, T_BANK):
-                sums = lag_sums(dtile, first_t)
+            for first_t in range(T_BANK, TM, T_BANK):
                 if more:
-                    own_latent_term(dtile + 1, first_t, rows)
-                add_lag_sums_and_store(dtile, first_t, sums)
-                if more:
-                    add_context(dtile + 1, first_t, rows)
+                    plain_terms(dtile + 1, first_t - T_BANK, rows)
+                lag_terms(dtile, first_t)
+            if more:
+                plain_terms(dtile + 1, TM - T_BANK, rows)

from contextlib import ExitStack

import concourse.mybir as mybir
from concourse.masks import make_identity

F32 = mybir.dt.float32
BF16 = mybir.dt.bfloat16
I32 = mybir.dt.int32
U32 = mybir.dt.uint32
U8 = mybir.dt.uint8
FP8X4 = mybir.dt.float8_e4m3fn_x4
ADD = mybir.AluOpType.add
MULT = mybir.AluOpType.mult

P = 128
B, T, D, H, L = 128, 10, 1024, 128, 2
TM = T - L
F = H + L * D + 1
F_PAD = 2192

PACK = 4
K_PASS = P * PACK
PASSES = D // K_PASS
HALVES = 2
PASS_WORDS = K_PASS // 2

BANK = 512
D_TILE = 256
D_TILES = D // D_TILE
BLOCKS = D_TILE // P
T_BANK = BANK // D_TILE
X_LOAD = T_BANK
X_ORDER = [L] + [s for s in range(0, T, X_LOAD) if s != L]

FLOPS = 2 * B * TM * D * L * D + 2 * B * D * H


def tile_npchangetransitionprior_pa_kernel(tc, x, emb, Wg, bg, out):
    nc = tc.nc
    with ExitStack() as stack:
        keep = stack.enter_context(tc.tile_pool(name="keep", bufs=1))
        x_stage = stack.enter_context(tc.tile_pool(name="x_stage", bufs=3))
        w_stage = stack.enter_context(tc.tile_pool(name="w_stage", bufs=2))
        psum_stage = stack.enter_context(tc.psum_pool(name="psum_stage", bufs=4))
        psum_lag = stack.enter_context(tc.psum_pool(name="psum_lag", bufs=4))

        ident_f32 = keep.tile([P, P], F32)
        make_identity(nc, ident_f32[:])
        ident_bf16 = keep.tile([P, P], BF16)
        make_identity(nc, ident_bf16[:])
        ones = keep.tile([P, P], BF16)
        nc.vector.memset(ones[:], 1.0)
        bias_rows = keep.tile([P, D], BF16)
        nc.vector.memset(bias_rows[:].bitcast(I32), 0)

        emb_sb = keep.tile([P, H], BF16)
        x_sb = keep.tile([P, T, D], BF16)
        w_sb = keep.tile([P, D // P, F_PAD], BF16)

        def load_w_tile(dtile):
            for block in range(dtile * BLOCKS, (dtile + 1) * BLOCKS):
                nc.sync.dma_start(out=w_sb[:, block, 0:F], in_=Wg[block * P : (block + 1) * P, :])

        nc.sync.dma_start(out=emb_sb[:], in_=emb)
        nc.sync.dma_start(out=bias_rows[0:1, :], in_=bg.rearrange("(o d) -> o d", o=1))
        load_w_tile(0)
        for s in X_ORDER:
            nc.sync.dma_start(out=x_sb[:, s : s + X_LOAD, :], in_=x[:, s : s + X_LOAD, :])
        for dtile in range(1, D_TILES):
            load_w_tile(dtile)

        x_codes = keep.tile([P, T - 1, PASSES * B], U32, align_bytes=64)
        x_scales = keep.tile([P, T - 1, PASSES * B], U8, align_bytes=64)
        w_codes = keep.tile([P, D_TILES, L * PASSES * D_TILE], U32, align_bytes=64)
        w_scales = keep.tile([P, D_TILES, L * PASSES * D_TILE], U8, align_bytes=64)
        embT = keep.tile([P, B], BF16)
        weT = keep.tile([P, D], BF16)
        res = keep.tile([P, TM, D], F32)

        def word_transposes(bank, words, first_word):
            for g in range(PASSES):
                for u in range(HALVES):
                    start = first_word + g * PASS_WORDS + u * P
                    nc.tensor.transpose(bank[:, g, u, :], words[:, start : start + P], ident_f32[:])

        def quantise_x_step(s):
            bank = psum_stage.tile([P, PASSES, HALVES, B], F32, tag="stage")
            word_transposes(bank, x_sb[:, s, :].bitcast(F32), 0)
            grouped = x_stage.tile([P, PASSES, B, PACK], BF16, align_bytes=64)
            nc.scalar.copy(out=grouped[:].bitcast(F32), in_=bank[:].rearrange("p g u b -> p g b u"))
            nc.vector.quantize_mx(
                out=x_codes[:, s, :].bitcast(FP8X4),
                scales=x_scales[:, s, :],
                in_=grouped[:].rearrange("p g b j -> p (g b j)"),
            )

        def quantise_w_tile(dtile):
            grouped = w_stage.tile([P, L, PASSES, D_TILE, PACK], BF16, align_bytes=64)
            grouped_words = grouped[:].bitcast(F32)
            for i in range(BLOCKS):
                words = w_sb[:, dtile * BLOCKS + i, :].bitcast(F32)
                for l in range(L):
                    bank = psum_stage.tile([P, PASSES, HALVES, P], F32, tag="stage")
                    word_transposes(bank, words, (H + l * D) // 2)
                    nc.scalar.copy(
                        out=grouped_words[:, l, :, i * P : (i + 1) * P, :],
                        in_=bank[:].rearrange("p g u d -> p g d u"),
                    )
            nc.vector.quantize_mx(
                out=w_codes[:, dtile, :].bitcast(FP8X4),
                scales=w_scales[:, dtile, :],
                in_=grouped[:].rearrange("p l g d j -> p (l g d j)"),
            )

        def row_terms(dtile):
            cols = slice(dtile * D_TILE, (dtile + 1) * D_TILE)
            weT_ps = psum_stage.tile([P, D_TILE], BF16, tag="stage")
            rows = psum_stage.tile([P, 2, D_TILE], F32, tag="stage")
            for i in range(BLOCKS):
                block = dtile * BLOCKS + i
                part = slice(i * P, (i + 1) * P)
                nc.tensor.transpose(weT_ps[:, part], w_sb[:, block, 0:H], ident_bf16[:])
                nc.tensor.matmul(
                    rows[:, 0, part],
                    lhsT=w_sb[:, block, F - 1 : F].to_broadcast([P, P]),
                    rhs=ident_bf16[:],
                    start=True,
                    stop=True,
                )
            nc.scalar.copy(out=weT[:, cols], in_=weT_ps[:])
            nc.tensor.matmul(rows[:, 1, :], lhsT=embT[:], rhs=weT[:, cols], start=True, stop=False)
            nc.tensor.matmul(rows[:, 1, :], lhsT=ones[:], rhs=bias_rows[:, cols], start=False, stop=True)
            return rows

        def plain_terms(dtile, first_t, rows):
            cols = slice(dtile * D_TILE, (dtile + 1) * D_TILE)
            steps = slice(first_t, first_t + T_BANK)
            nc.vector.tensor_tensor(
                out=res[:, steps, cols],
                in0=x_sb[:, L + first_t : L + first_t + T_BANK, cols],
                in1=rows[:, 0:1, :].to_broadcast([P, T_BANK, D_TILE]),
                op=MULT,
            )
            nc.vector.tensor_tensor(
                out=res[:, steps, cols],
                in0=res[:, steps, cols],
                in1=rows[:, 1:2, :].to_broadcast([P, T_BANK, D_TILE]),
                op=ADD,
            )

        def lag_terms(dtile, first_t):
            cols = slice(dtile * D_TILE, (dtile + 1) * D_TILE)
            steps = slice(first_t, first_t + T_BANK)
            sums = psum_lag.tile([P, T_BANK, D_TILE], F32)
            for i in range(T_BANK):
                for l in range(L):
                    for g in range(PASSES):
                        series = slice(g * B, (g + 1) * B)
                        latents = slice((l * PASSES + g) * D_TILE, (l * PASSES + g + 1) * D_TILE)
                        nc.tensor.matmul_mx(
                            out=sums[:, i, :],
                            lhsT=x_codes[:, first_t + i + l, series].bitcast(FP8X4),
                            lhsT_scale=x_scales[:, first_t + i + l, series],
                            rhs=w_codes[:, dtile, latents].bitcast(FP8X4),
                            rhs_scale=w_scales[:, dtile, latents],
                            start=(l == 0 and g == 0),
                            stop=(l == L - 1 and g == PASSES - 1),
                        )
            nc.vector.tensor_tensor(out=res[:, steps, cols], in0=sums[:], in1=res[:, steps, cols], op=ADD)
            nc.sync.dma_start(out=out[:, steps, cols], in_=res[:, steps, cols])

        embT_ps = psum_stage.tile([P, B], BF16, tag="stage")
        nc.tensor.transpose(embT_ps[:], emb_sb[:], ident_bf16[:])
        nc.scalar.copy(out=embT[:], in_=embT_ps[:])

        rows = row_terms(0)
        quantise_w_tile(0)
        for s in X_ORDER:
            if s >= L:
                plain_terms(0, s - L, rows)
            for step in range(s, min(s + X_LOAD, T - 1)):
                quantise_x_step(step)
        for dtile in range(D_TILES):
            more = dtile + 1 < D_TILES
            lag_terms(dtile, 0)
            if more:
                quantise_w_tile(dtile + 1)
                rows = row_terms(dtile + 1)
            for first_t in range(T_BANK, TM, T_BANK):
                if more:
                    plain_terms(dtile + 1, first_t - T_BANK, rows)
                lag_terms(dtile, first_t)
            if more:
                plain_terms(dtile + 1, TM - T_BANK, rows)
